import numpy as np
import ml_dtypes


def mxq(x, axis, fmt="e4m3"):
    dtype, down = {"e4m3": (ml_dtypes.float8_e4m3fn, 7), "e5m2": (ml_dtypes.float8_e5m2, 14)}[fmt]
    v = np.moveaxis(np.asarray(x, np.float32).astype(ml_dtypes.bfloat16).astype(np.float64), axis, -1)
    blocks = v.reshape(v.shape[:-1] + (-1, 32))
    amax = np.abs(blocks).max(-1, keepdims=True)
    byte = np.maximum(np.where(amax > 0, np.frexp(amax)[1] - 1 + 127, 0) - down, 1)
    scale = np.exp2(byte - 127.0)
    codes = (blocks / scale).astype(np.float32).astype(dtype).astype(np.float64)
    return np.moveaxis((codes * scale).reshape(v.shape), -1, axis)


WIDE = False


def mx_kscale(k):
    if not WIDE:
        return np.ones(k)
    levels = np.array([10, -10, 5, -5, 0])
    if k % 512:
        return np.exp2(np.random.permutation(np.resize(levels, k // 32))).repeat(32)
    a = np.empty((k // 512, 16))
    for p in range(k // 512):
        a[p, :8] = np.random.permutation(np.resize(levels, 8))
        for g in range(8):
            far = levels[np.abs(levels - a[p, g]) >= 10]
            a[p, g + 8] = far[np.random.randint(len(far))]
    return np.exp2(a.ravel()).repeat(32)


BF16 = ml_dtypes.bfloat16


def bf(x):
    return np.asarray(x, np.float32).astype(BF16)


def f64(x):
    return np.asarray(x).astype(np.float64)


B, S, H, NH, NKV, HD = 2, 512, 2048, 16, 4, 128
EPS = 1e-6


def rms_norm(x, w):
    var = np.mean(x * x, axis=-1, keepdims=True)
    return x * (1.0 / np.sqrt(var + EPS)) * w


def rotate_half(x):
    x1, x2 = np.split(x, 2, axis=-1)
    return np.concatenate([-x2, x1], axis=-1)


def setup_inputs():
    s = mx_kscale(H)
    inv_freq = 1.0 / (10000.0 ** (np.arange(0, HD, 2) / HD))
    freqs = np.arange(S)[:, None] * inv_freq[None, :]
    emb = np.concatenate([freqs, freqs], axis=-1)
    return {"hidden_states": bf(np.random.standard_normal((B, S, H)) * s),
            "cos": bf(np.cos(emb)),
            "sin": bf(np.sin(emb)),
            "wq": bf(np.random.standard_normal((NH * HD, H)) / np.sqrt(H) / s[None, :]),
            "wk": bf(np.random.standard_normal((NKV * HD, H)) / np.sqrt(H) / s[None, :]),
            "q_norm_w": bf(1.0 + 0.1 * np.random.standard_normal(HD)),
            "k_norm_w": bf(1.0 + 0.1 * np.random.standard_normal(HD)),
            "ssmax_scale": bf((1.0 + 0.2 * np.random.standard_normal((1, NH, 1, 1))) / np.log(S))}


def reference(hidden_states, cos, sin, wq, wk, q_norm_w, k_norm_w, ssmax_scale):
    xq = mxq(f64(hidden_states), 2, "e4m3")
    q = (xq @ mxq(f64(wq), 1, "e4m3").T).reshape(B, S, NH, HD)
    k = (xq @ mxq(f64(wk), 1, "e4m3").T).reshape(B, S, NKV, HD)
    q = rms_norm(q, f64(q_norm_w)).transpose(0, 2, 1, 3)
    k = rms_norm(k, f64(k_norm_w)).transpose(0, 2, 1, 3)
    c = f64(cos)[None, None]
    sn = f64(sin)[None, None]
    q = q * c + rotate_half(q) * sn
    k = k * c + rotate_half(k) * sn
    q = q * (f64(ssmax_scale) * np.log(S))
    return q, k

@@ -1,0 +1,247 @@
+from contextlib import ExitStack
+import math
+
+import concourse.mybir as mybir
+from concourse.masks import make_identity
+
+F32 = mybir.dt.float32
+BF16 = mybir.dt.bfloat16
+U32 = mybir.dt.uint32
+U8 = mybir.dt.uint8
+FP8X4 = mybir.dt.float8_e4m3fn_x4
+ACT = mybir.ActivationFunctionType
+ALU = mybir.AluOpType
+
+P = 128
+BATCH, SEQ, HIDDEN = 2, 512, 2048
+Q_HEADS, KV_HEADS, HEAD_DIM = 16, 4, 128
+HALF = HEAD_DIM // 2
+EPS = 1e-6
+
+K_PASS = 4 * P
+PASSES = HIDDEN // K_PASS
+WORDS_PER_PASS = K_PASS // 2
+SEQ_TILES = SEQ // P
+TOKEN_TILES = BATCH * SEQ_TILES
+CHUNK_HEADS = 4
+CHUNK = CHUNK_HEADS * HEAD_DIM
+Q_CHUNKS = Q_HEADS // CHUNK_HEADS
+CHUNKS = Q_CHUNKS + KV_HEADS // CHUNK_HEADS
+HEADS = Q_HEADS + KV_HEADS
+ROW_TILES = TOKEN_TILES + CHUNKS * CHUNK_HEADS
+
+X_LEAD = 2
+GPSIMD_TILES = 3
+
+FLOPS = 2 * BATCH * SEQ * HIDDEN * HEADS * HEAD_DIM
+
+
+def tile_biboattention_pa_kernel(
+    tc, hidden_states, cos, sin, wq, wk, q_norm_w, k_norm_w, ssmax_scale, out_0, out_1
+):
+    nc = tc.nc
+    with ExitStack() as ctx:
+        const = ctx.enter_context(tc.tile_pool(name="const", bufs=1))
+        raw_pool = ctx.enter_context(tc.tile_pool(name="raw", bufs=ROW_TILES))
+        grouped_pool = ctx.enter_context(tc.tile_pool(name="grouped", bufs=3))
+        w_pool = ctx.enter_context(tc.tile_pool(name="w_mx", bufs=3))
+        small = ctx.enter_context(tc.tile_pool(name="small", bufs=4))
+        prod_pool = ctx.enter_context(tc.tile_pool(name="prod", bufs=3))
+        result_pool = ctx.enter_context(tc.tile_pool(name="result", bufs=3))
+        flip_psum = ctx.enter_context(tc.psum_pool(name="flip_psum", bufs=4))
+        acc_psum = ctx.enter_context(tc.psum_pool(name="acc_psum", bufs=4))
+        ctx.enter_context(tc.manual_schedule())
+
+        x_view = hidden_states.rearrange("b (p t) k -> b t p k", t=SEQ_TILES)
+        wq_view = wq.rearrange("(n j p) k -> n j p k", j=CHUNK_HEADS, p=P)
+        wk_view = wk.rearrange("(j p) k -> j p k", p=P)
+
+        def lead_in(on_x, on_w):
+            for j in range(CHUNK_HEADS):
+                on_w(0, j)
+            for m in range(X_LEAD):
+                on_x(m)
+
+        def all_banks(on_x, on_w, on_bank):
+            for n in range(CHUNKS):
+                for m in range(TOKEN_TILES):
+                    if n == 0 and m + X_LEAD < TOKEN_TILES:
+                        on_x(m + X_LEAD)
+                    if n + 1 < CHUNKS and m < CHUNK_HEADS:
+                        on_w(n + 1, m)
+                    on_bank(m, n)
+
+        x_raw = {}
+        w_raw = {}
+
+        def load_x(m):
+            x_raw[m] = raw_pool.tile([P, HIDDEN], BF16, name="raw")
+            nc.sync.dma_start(out=x_raw[m][:], in_=x_view[m // SEQ_TILES, m % SEQ_TILES])
+
+        def load_w(n, j):
+            w_raw[n, j] = raw_pool.tile([P, HIDDEN], BF16, name="raw")
+            nc.sync.dma_start(out=w_raw[n, j][:], in_=wq_view[n, j] if n < Q_CHUNKS else wk_view[j])
+
+        lead_in(load_x, load_w)
+        all_banks(load_x, load_w, lambda m, n: None)
+
+        cos_sb = const.tile([P, SEQ_TILES, HEAD_DIM], BF16)
+        sin_sb = const.tile([P, SEQ_TILES, HEAD_DIM], BF16)
+        nc.scalar.dma_start(out=cos_sb[:], in_=cos.rearrange("(p t) d -> p t d", t=SEQ_TILES))
+        nc.scalar.dma_start(out=sin_sb[:], in_=sin.rearrange("(p t) d -> p t d", t=SEQ_TILES))
+        vectors = const.tile([P, CHUNK], BF16)
+        nc.vector.memset(vectors[:], 0.0)
+        ones = const.tile([P, P], BF16)
+        nc.vector.memset(ones[:], 1.0)
+        nc.scalar.dma_start(out=vectors[0:1, 0:HEAD_DIM], in_=q_norm_w.unsqueeze(0))
+        nc.scalar.dma_start(out=vectors[0:1, HEAD_DIM : 2 * HEAD_DIM], in_=k_norm_w.unsqueeze(0))
+        nc.scalar.dma_start(
+            out=vectors[0:1, 2 * HEAD_DIM : 2 * HEAD_DIM + Q_HEADS],
+            in_=ssmax_scale.rearrange("a h b c -> (a b c) h"),
+        )
+        ident = const.tile([P, P], F32)
+        make_identity(nc, ident[:])
+
+        one = const.tile([P, 1], F32)
+        nc.vector.memset(one[:], 1.0)
+        warm = const.tile([P, 1], F32)
+        nc.scalar.activation(out=warm[:], in_=one[:], func=ACT.Abs_reciprocal_sqrt)
+
+        gain = const.tile([P, HEADS], F32)
+        table = const.tile([P, SEQ_TILES, 2, 2, HEAD_DIM], F32)
+
+        def build_tables():
+          spread = flip_psum.tile([P, CHUNK], F32, name="flipped")
+          nc.tensor.matmul(out=spread[:], lhsT=ones[:], rhs=vectors[:], start=True, stop=True)
+          norm_w = spread[:, : 2 * HEAD_DIM].rearrange("p (kind d) -> p kind d", kind=2)
+          nc.vector.memset(gain[:, Q_HEADS:], 1.0)
+          nc.vector.tensor_scalar_mul(out=gain[:, :Q_HEADS], in0=spread[:, 2 * HEAD_DIM : 2 * HEAD_DIM + Q_HEADS], scalar1=math.log(SEQ))
+          for kind in range(2):
+              nc.vector.tensor_tensor(
+                  out=table[:, :, kind, 0, :],
+                  in0=cos_sb[:],
+                  in1=norm_w[:, kind, :].unsqueeze(1).to_broadcast([P, SEQ_TILES, HEAD_DIM]),
+                  op=ALU.mult,
+              )
+              nc.vector.tensor_tensor(
+                  out=table[:, :, kind, 1, :HALF],
+                  in0=sin_sb[:, :, HALF:],
+                  in1=norm_w[:, kind, :HALF].unsqueeze(1).to_broadcast([P, SEQ_TILES, HALF]),
+                  op=ALU.mult,
+              )
+              nc.vector.scalar_tensor_tensor(
+                  out=table[:, :, kind, 1, HALF:],
+                  in0=sin_sb[:, :, :HALF],
+                  scalar=-1.0,
+                  in1=norm_w[:, kind, HALF:].unsqueeze(1).to_broadcast([P, SEQ_TILES, HALF]),
+                  op0=ALU.mult,
+                  op1=ALU.mult,
+              )
+
+        x_codes = const.tile([P, TOKEN_TILES, PASSES, P], U32, align_bytes=64)
+        x_scales = const.tile([P, TOKEN_TILES, PASSES, P], U8, align_bytes=64)
+
+        def quantise_row_tile(raw, codes, scales):
+            words = raw[:].bitcast(F32)
+            grouped = grouped_pool.tile([P, PASSES, P, 2], F32, align_bytes=64)
+            for bank in range(PASSES // 2):
+                flipped = flip_psum.tile([P, 2, 2, P], F32)
+                for a in range(2):
+                    for u in range(2):
+                        first = (2 * bank + a) * WORDS_PER_PASS
+                        nc.tensor.transpose(
+                            flipped[:, a, u, :], words[:, first + u : first + WORDS_PER_PASS : 2], ident[:]
+                        )
+                nc.scalar.copy(
+                    out=grouped[:, 2 * bank : 2 * bank + 2, :, :],
+                    in_=flipped[:].rearrange("p a u r -> p a r u"),
+                )
+            for g in range(PASSES):
+                nc.vector.quantize_mx(
+                    out=codes[:, g, :].bitcast(FP8X4),
+                    scales=scales[:, g, :],
+                    in_=grouped[:, g, :, :].rearrange("p r u -> p (r u)").bitcast(BF16),
+                )
+
+        w_mx = {}
+
+        def prepare_w(n, j):
+            if j == 0:
+                w_codes = w_pool.tile([P, PASSES, CHUNK], U32, align_bytes=64)
+                w_scales = w_pool.tile([P, PASSES, CHUNK], U8, align_bytes=64)
+                w_mx[n] = (w_codes, w_scales)
+            w_codes, w_scales = w_mx[n]
+            rows = slice(j * P, (j + 1) * P)
+            quantise_row_tile(w_raw[n, j], w_codes[:, :, rows], w_scales[:, :, rows])
+
+        def prepare_x(m):
+            quantise_row_tile(x_raw[m], x_codes[:, m], x_scales[:, m])
+
+        results = {}
+
+        def project(m, n):
+            b, t = m // SEQ_TILES, m % SEQ_TILES
+            kind = 0 if n < Q_CHUNKS else 1
+            w_codes, w_scales = w_mx[n]
+            acc = acc_psum.tile([P, CHUNK], F32)
+            for g in range(PASSES):
+                nc.tensor.matmul_mx(
+                    out=acc[:],
+                    lhsT=x_codes[:, m, g, :].bitcast(FP8X4),
+                    lhsT_scale=x_scales[:, m, g, :],
+                    rhs=w_codes[:, g, :].bitcast(FP8X4),
+                    rhs_scale=w_scales[:, g, :],
+                    start=(g == 0),
+                    stop=(g == PASSES - 1),
+                )
+            sumsq = small.tile([P, CHUNK_HEADS], F32)
+            for h in range(CHUNK_HEADS):
+                squares = small.tile([P, HEAD_DIM], F32)
+                nc.scalar.activation(
+                    out=squares[:],
+                    in_=acc[:, h * HEAD_DIM : (h + 1) * HEAD_DIM],
+                    func=ACT.Square,
+                    accum_out=sumsq[:, h : h + 1],
+                )
+            rstd = small.tile([P, CHUNK_HEADS], F32)
+            nc.scalar.activation(
+                out=rstd[:], in_=sumsq[:], func=ACT.Abs_reciprocal_sqrt, scale=1.0 / HEAD_DIM, bias=EPS
+            )
+            factor = small.tile([P, CHUNK_HEADS], F32)
+            nc.vector.tensor_mul(
+                out=factor[:], in0=rstd[:], in1=gain[:, n * CHUNK_HEADS : (n + 1) * CHUNK_HEADS]
+            )
+            prod = prod_pool.tile([P, CHUNK_HEADS, 2, HEAD_DIM], F32)
+            for h in range(CHUNK_HEADS):
+                nc.vector.scalar_tensor_tensor(
+                    out=prod[:, h, :, :],
+                    in0=table[:, t, kind, :, :],
+                    scalar=factor[:, h : h + 1],
+                    in1=acc[:, h * HEAD_DIM : (h + 1) * HEAD_DIM].unsqueeze(1).to_broadcast([P, 2, HEAD_DIM]),
+                    op0=ALU.mult,
+                    op1=ALU.mult,
+                )
+            if t == 0:
+                result = result_pool.tile([P, CHUNK_HEADS, SEQ_TILES, HEAD_DIM], F32)
+                results[0] = result
+            result = results[0]
+            adder = nc.gpsimd if t < GPSIMD_TILES else nc.vector
+            adder.tensor_tensor(
+                out=result[:, :, t, :HALF], in0=prod[:, :, 0, :HALF], in1=prod[:, :, 1, HALF:], op=ALU.add
+            )
+            adder.tensor_tensor(
+                out=result[:, :, t, HALF:], in0=prod[:, :, 0, HALF:], in1=prod[:, :, 1, :HALF], op=ALU.add
+            )
+            if kind == 0:
+                heads = out_0[b, n * CHUNK_HEADS : (n + 1) * CHUNK_HEADS]
+            else:
+                heads = out_1[b]
+            rows = heads.rearrange("h (p t) d -> p h t d", t=SEQ_TILES)
+            if t == GPSIMD_TILES - 1:
+                nc.sync.dma_start(out=rows[:, :, :GPSIMD_TILES, :], in_=result[:, :, :GPSIMD_TILES, :])
+            if t == SEQ_TILES - 1:
+                nc.sync.dma_start(out=rows[:, :, GPSIMD_TILES:, :], in_=result[:, :, GPSIMD_TILES:, :])
+
+        lead_in(prepare_x, prepare_w)
+        build_tables()
+        all_banks(prepare_x, prepare_w, project)

@@ -30,8 +30,9 @@ CHUNKS = Q_CHUNKS + KV_HEADS // CHUNK_HEADS
 HEADS = Q_HEADS + KV_HEADS
 ROW_TILES = TOKEN_TILES + CHUNKS * CHUNK_HEADS
 
-X_LEAD = 2
-GPSIMD_TILES = 3
+PAIR = 2
+PAIRS_PER_CHUNK = TOKEN_TILES // PAIR
+PAIRS = CHUNKS * PAIRS_PER_CHUNK
 
 FLOPS = 2 * BATCH * SEQ * HIDDEN * HEADS * HEAD_DIM
 
@@ -43,7 +44,7 @@ def tile_biboattention_pa_kernel(
     with ExitStack() as ctx:
         const = ctx.enter_context(tc.tile_pool(name="const", bufs=1))
         raw_pool = ctx.enter_context(tc.tile_pool(name="raw", bufs=ROW_TILES))
-        grouped_pool = ctx.enter_context(tc.tile_pool(name="grouped", bufs=3))
+        grouped_pool = ctx.enter_context(tc.tile_pool(name="grouped", bufs=4))
         w_pool = ctx.enter_context(tc.tile_pool(name="w_mx", bufs=3))
         small = ctx.enter_context(tc.tile_pool(name="small", bufs=4))
         prod_pool = ctx.enter_context(tc.tile_pool(name="prod", bufs=3))
@@ -56,34 +57,35 @@ def tile_biboattention_pa_kernel(
         wq_view = wq.rearrange("(n j p) k -> n j p k", j=CHUNK_HEADS, p=P)
         wk_view = wk.rearrange("(j p) k -> j p k", p=P)
 
-        def lead_in(on_x, on_w):
-            for j in range(CHUNK_HEADS):
-                on_w(0, j)
-            for m in range(X_LEAD):
-                on_x(m)
+        lead_in = [("w", 0, j) for j in range(CHUNK_HEADS)] + [("x", m) for m in range(PAIR)]
 
-        def all_banks(on_x, on_w, on_bank):
-            for n in range(CHUNKS):
-                for m in range(TOKEN_TILES):
-                    if n == 0 and m + X_LEAD < TOKEN_TILES:
-                        on_x(m + X_LEAD)
-                    if n + 1 < CHUNKS and m < CHUNK_HEADS:
-                        on_w(n + 1, m)
-                    on_bank(m, n)
+        def made_ready_in(pair):
+            n, i = divmod(pair, PAIRS_PER_CHUNK)
+            tiles = []
+            if n == 0 and i + 1 < PAIRS_PER_CHUNK:
+                tiles += [("x", (i + 1) * PAIR + m) for m in range(PAIR)]
+            if n + 1 < CHUNKS:
+                tiles.append(("w", n + 1, i))
+            return tiles
 
-        x_raw = {}
-        w_raw = {}
+        raws = {}
 
-        def load_x(m):
-            x_raw[m] = raw_pool.tile([P, HIDDEN], BF16, name="raw")
-            nc.sync.dma_start(out=x_raw[m][:], in_=x_view[m // SEQ_TILES, m % SEQ_TILES])
+        def load(tile):
+            raw = raw_pool.tile([P, HIDDEN], BF16, name="raw")
+            if tile[0] == "x":
+                source = x_view[tile[1] // SEQ_TILES, tile[1] % SEQ_TILES]
+            elif tile[1] < Q_CHUNKS:
+                source = wq_view[tile[1], tile[2]]
+            else:
+                source = wk_view[tile[2]]
+            nc.sync.dma_start(out=raw[:], in_=source)
+            raws[tile] = raw
 
-        def load_w(n, j):
-            w_raw[n, j] = raw_pool.tile([P, HIDDEN], BF16, name="raw")
-            nc.sync.dma_start(out=w_raw[n, j][:], in_=wq_view[n, j] if n < Q_CHUNKS else wk_view[j])
-
-        lead_in(load_x, load_w)
-        all_banks(load_x, load_w, lambda m, n: None)
+        for tile in lead_in:
+            load(tile)
+        for pair in range(PAIRS):
+            for tile in made_ready_in(pair):
+                load(tile)
 
         cos_sb = const.tile([P, SEQ_TILES, HEAD_DIM], BF16)
         sin_sb = const.tile([P, SEQ_TILES, HEAD_DIM], BF16)
@@ -141,107 +143,175 @@ def tile_biboattention_pa_kernel(
         x_codes = const.tile([P, TOKEN_TILES, PASSES, P], U32, align_bytes=64)
         x_scales = const.tile([P, TOKEN_TILES, PASSES, P], U8, align_bytes=64)
 
-        def quantise_row_tile(raw, codes, scales):
-            words = raw[:].bitcast(F32)
-            grouped = grouped_pool.tile([P, PASSES, P, 2], F32, align_bytes=64)
-            for bank in range(PASSES // 2):
-                flipped = flip_psum.tile([P, 2, 2, P], F32)
+        w_mx = {}
+        banks = {}
+        grouped_of = {}
+
+        def turn(tile):
+            words = raws[tile][:].bitcast(F32)
+            for half in range(2):
+                flipped = flip_psum.tile([P, 2, 2, P], F32, name="flipped")
                 for a in range(2):
+                    first = (2 * half + a) * WORDS_PER_PASS
                     for u in range(2):
-                        first = (2 * bank + a) * WORDS_PER_PASS
                         nc.tensor.transpose(
                             flipped[:, a, u, :], words[:, first + u : first + WORDS_PER_PASS : 2], ident[:]
                         )
-                nc.scalar.copy(
-                    out=grouped[:, 2 * bank : 2 * bank + 2, :, :],
-                    in_=flipped[:].rearrange("p a u r -> p a r u"),
-                )
-            for g in range(PASSES):
-                nc.vector.quantize_mx(
-                    out=codes[:, g, :].bitcast(FP8X4),
-                    scales=scales[:, g, :],
-                    in_=grouped[:, g, :, :].rearrange("p r u -> p (r u)").bitcast(BF16),
-                )
+                banks[tile, half] = flipped
 
-        w_mx = {}
+        def group(tile, half):
+            if half == 0:
+                grouped = grouped_pool.tile([P, PASSES, P, 2], F32, align_bytes=64)
+                grouped_of[tile] = grouped
+            nc.scalar.copy(
+                out=grouped_of[tile][:, 2 * half : 2 * half + 2, :, :],
+                in_=banks[tile, half][:].rearrange("p a u r -> p a r u"),
+            )
 
-        def prepare_w(n, j):
+        def quantise(tile):
+            grouped = grouped_of[tile]
+            if tile[0] == "x":
+                for g in range(0, PASSES, 2):
+                    nc.vector.quantize_mx(
+                        out=x_codes[:, tile[1], g : g + 2, :].rearrange("p g r -> p (g r)").bitcast(FP8X4),
+                        scales=x_scales[:, tile[1], g : g + 2, :].rearrange("p g r -> p (g r)"),
+                        in_=grouped[:, g : g + 2, :, :].rearrange("p g r u -> p (g r u)").bitcast(BF16),
+                    )
+                return
+            n, j = tile[1], tile[2]
             if j == 0:
                 w_codes = w_pool.tile([P, PASSES, CHUNK], U32, align_bytes=64)
                 w_scales = w_pool.tile([P, PASSES, CHUNK], U8, align_bytes=64)
                 w_mx[n] = (w_codes, w_scales)
             w_codes, w_scales = w_mx[n]
             rows = slice(j * P, (j + 1) * P)
-            quantise_row_tile(w_raw[n, j], w_codes[:, :, rows], w_scales[:, :, rows])
+            for g in range(PASSES):
+                nc.vector.quantize_mx(
+                    out=w_codes[:, g, rows].bitcast(FP8X4),
+                    scales=w_scales[:, g, rows],
+                    in_=grouped[:, g, :, :].rearrange("p r u -> p (r u)").bitcast(BF16),
+                )
 
-        def prepare_x(m):
-            quantise_row_tile(x_raw[m], x_codes[:, m], x_scales[:, m])
+        def tiles_of(pair):
+            n, i = divmod(pair, PAIRS_PER_CHUNK)
+            return n, [i * PAIR + m for m in range(PAIR)]
 
+        accs = {}
+        sums = {}
+        factors = {}
+        prods = {}
         results = {}
 
-        def project(m, n):
-            b, t = m // SEQ_TILES, m % SEQ_TILES
-            kind = 0 if n < Q_CHUNKS else 1
+        def project(pair):
+            n, ms = tiles_of(pair)
             w_codes, w_scales = w_mx[n]
-            acc = acc_psum.tile([P, CHUNK], F32)
-            for g in range(PASSES):
-                nc.tensor.matmul_mx(
-                    out=acc[:],
-                    lhsT=x_codes[:, m, g, :].bitcast(FP8X4),
-                    lhsT_scale=x_scales[:, m, g, :],
-                    rhs=w_codes[:, g, :].bitcast(FP8X4),
-                    rhs_scale=w_scales[:, g, :],
-                    start=(g == 0),
-                    stop=(g == PASSES - 1),
-                )
-            sumsq = small.tile([P, CHUNK_HEADS], F32)
-            for h in range(CHUNK_HEADS):
-                squares = small.tile([P, HEAD_DIM], F32)
-                nc.scalar.activation(
-                    out=squares[:],
-                    in_=acc[:, h * HEAD_DIM : (h + 1) * HEAD_DIM],
-                    func=ACT.Square,
-                    accum_out=sumsq[:, h : h + 1],
-                )
-            rstd = small.tile([P, CHUNK_HEADS], F32)
+            for m in ms:
+                acc = acc_psum.tile([P, CHUNK], F32)
+                for g in range(PASSES):
+                    nc.tensor.matmul_mx(
+                        out=acc[:],
+                        lhsT=x_codes[:, m, g, :].bitcast(FP8X4),
+                        lhsT_scale=x_scales[:, m, g, :],
+                        rhs=w_codes[:, g, :].bitcast(FP8X4),
+                        rhs_scale=w_scales[:, g, :],
+                        start=(g == 0),
+                        stop=(g == PASSES - 1),
+                    )
+                accs[m, n] = acc
+
+        def square_sums(pair):
+            n, ms = tiles_of(pair)
+            sumsq = small.tile([P, PAIR, CHUNK_HEADS], F32)
+            for i, m in enumerate(ms):
+                for h in range(CHUNK_HEADS):
+                    squares = small.tile([P, HEAD_DIM], F32)
+                    nc.scalar.activation(
+                        out=squares[:],
+                        in_=accs[m, n][:, h * HEAD_DIM : (h + 1) * HEAD_DIM],
+                        func=ACT.Square,
+                        accum_out=sumsq[:, i, h : h + 1],
+                    )
+            sums[pair] = sumsq
+
+        def make_factors(pair):
+            n, ms = tiles_of(pair)
+            rstd = small.tile([P, PAIR, CHUNK_HEADS], F32)
             nc.scalar.activation(
-                out=rstd[:], in_=sumsq[:], func=ACT.Abs_reciprocal_sqrt, scale=1.0 / HEAD_DIM, bias=EPS
+                out=rstd[:], in_=sums[pair][:], func=ACT.Abs_reciprocal_sqrt, scale=1.0 / HEAD_DIM, bias=EPS
             )
-            factor = small.tile([P, CHUNK_HEADS], F32)
-            nc.vector.tensor_mul(
-                out=factor[:], in0=rstd[:], in1=gain[:, n * CHUNK_HEADS : (n + 1) * CHUNK_HEADS]
+            factor = small.tile([P, PAIR, CHUNK_HEADS], F32)
+            nc.gpsimd.tensor_tensor(
+                out=factor[:],
+                in0=rstd[:],
+                in1=gain[:, n * CHUNK_HEADS : (n + 1) * CHUNK_HEADS].unsqueeze(1).to_broadcast([P, PAIR, CHUNK_HEADS]),
+                op=ALU.mult,
             )
-            prod = prod_pool.tile([P, CHUNK_HEADS, 2, HEAD_DIM], F32)
+            factors[pair] = factor
+
+        def multiply(pair, i):
+            n, ms = tiles_of(pair)
+            kind = 0 if n < Q_CHUNKS else 1
+            acc = accs[ms[i], n]
+            prod = prod_pool.tile([P, CHUNK_HEADS, 2, 2, HALF], F32)
             for h in range(CHUNK_HEADS):
                 nc.vector.scalar_tensor_tensor(
-                    out=prod[:, h, :, :],
-                    in0=table[:, t, kind, :, :],
-                    scalar=factor[:, h : h + 1],
+                    out=prod[:, h, :, :, :].rearrange("p k a d -> p k (a d)"),
+                    in0=table[:, ms[i] % SEQ_TILES, kind, :, :],
+                    scalar=factors[pair][:, i, h : h + 1],
                     in1=acc[:, h * HEAD_DIM : (h + 1) * HEAD_DIM].unsqueeze(1).to_broadcast([P, 2, HEAD_DIM]),
                     op0=ALU.mult,
                     op1=ALU.mult,
                 )
+            prods[pair, i] = prod
+
+        def add_and_store(pair, i):
+            n, ms = tiles_of(pair)
+            b, t = divmod(ms[i], SEQ_TILES)
             if t == 0:
-                result = result_pool.tile([P, CHUNK_HEADS, SEQ_TILES, HEAD_DIM], F32)
+                result = result_pool.tile([P, CHUNK_HEADS, SEQ_TILES, 2, HALF], F32)
                 results[0] = result
             result = results[0]
-            adder = nc.gpsimd if t < GPSIMD_TILES else nc.vector
-            adder.tensor_tensor(
-                out=result[:, :, t, :HALF], in0=prod[:, :, 0, :HALF], in1=prod[:, :, 1, HALF:], op=ALU.add
+            prod = prods[pair, i]
+            nc.gpsimd.tensor_tensor(
+                out=result[:, :, t, :, :], in0=prod[:, :, 0, :, :], in1=prod[:, :, 1, ::-1, :], op=ALU.add
             )
-            adder.tensor_tensor(
-                out=result[:, :, t, HALF:], in0=prod[:, :, 0, HALF:], in1=prod[:, :, 1, :HALF], op=ALU.add
-            )
-            if kind == 0:
-                heads = out_0[b, n * CHUNK_HEADS : (n + 1) * CHUNK_HEADS]
-            else:
-                heads = out_1[b]
+            heads = out_0[b, n * CHUNK_HEADS : (n + 1) * CHUNK_HEADS] if n < Q_CHUNKS else out_1[b]
             rows = heads.rearrange("h (p t) d -> p h t d", t=SEQ_TILES)
-            if t == GPSIMD_TILES - 1:
-                nc.sync.dma_start(out=rows[:, :, :GPSIMD_TILES, :], in_=result[:, :, :GPSIMD_TILES, :])
-            if t == SEQ_TILES - 1:
-                nc.sync.dma_start(out=rows[:, :, GPSIMD_TILES:, :], in_=result[:, :, GPSIMD_TILES:, :])
+            last = pair == PAIRS - 1
+            if last or i == PAIR - 1:
+                first = t if last else t - 1
+                nc.sync.dma_start(
+                    out=rows[:, :, first : t + 1, :],
+                    in_=result[:, :, first : t + 1, :, :].rearrange("p h t a d -> p h t (a d)"),
+                )
 
-        lead_in(prepare_x, prepare_w)
+        for tile in lead_in:
+            turn(tile)
+            group(tile, 0)
+            group(tile, 1)
+            quantise(tile)
         build_tables()
-        all_banks(prepare_x, prepare_w, project)
+        for pair in range(PAIRS + 1):
+            ready = made_ready_in(pair) if pair < PAIRS else []
+            for tile in ready:
+                turn(tile)
+                group(tile, 0)
+                if tile == ready[0] and pair > 0:
+                    make_factors(pair - 1)
+                group(tile, 1)
+            if not ready:
+                make_factors(pair - 1)
+            if pair > 0:
+                multiply(pair - 1, 0)
+            for tile in ready[:1]:
+                quantise(tile)
+            if pair > 0:
+                add_and_store(pair - 1, 0)
+                multiply(pair - 1, 1)
+            for tile in ready[1:]:
+                quantise(tile)
+            if pair > 0:
+                add_and_store(pair - 1, 1)
+            if pair < PAIRS:
+                project(pair)
+                square_sums(pair)

@@ -30,9 +30,10 @@ CHUNKS = Q_CHUNKS + KV_HEADS // CHUNK_HEADS
 HEADS = Q_HEADS + KV_HEADS
 ROW_TILES = TOKEN_TILES + CHUNKS * CHUNK_HEADS
 
-PAIR = 2
-PAIRS_PER_CHUNK = TOKEN_TILES // PAIR
-PAIRS = CHUNKS * PAIRS_PER_CHUNK
+X_LEAD = 2
+RUN = 2
+BANKS = CHUNKS * TOKEN_TILES
+ADD_LAG = 2
 
 FLOPS = 2 * BATCH * SEQ * HIDDEN * HEADS * HEAD_DIM
 
@@ -45,7 +46,7 @@ def tile_biboattention_pa_kernel(
         const = ctx.enter_context(tc.tile_pool(name="const", bufs=1))
         raw_pool = ctx.enter_context(tc.tile_pool(name="raw", bufs=ROW_TILES))
         grouped_pool = ctx.enter_context(tc.tile_pool(name="grouped", bufs=4))
-        w_pool = ctx.enter_context(tc.tile_pool(name="w_mx", bufs=3))
+        w_pool = ctx.enter_context(tc.tile_pool(name="w_mx", bufs=2))
         small = ctx.enter_context(tc.tile_pool(name="small", bufs=4))
         prod_pool = ctx.enter_context(tc.tile_pool(name="prod", bufs=3))
         result_pool = ctx.enter_context(tc.tile_pool(name="result", bufs=3))
@@ -57,15 +58,19 @@ def tile_biboattention_pa_kernel(
         wq_view = wq.rearrange("(n j p) k -> n j p k", j=CHUNK_HEADS, p=P)
         wk_view = wk.rearrange("(j p) k -> j p k", p=P)
 
-        lead_in = [("w", 0, j) for j in range(CHUNK_HEADS)] + [("x", m) for m in range(PAIR)]
+        lead_in = [("w", 0, j) for j in range(CHUNK_HEADS)] + [("x", m) for m in range(X_LEAD)]
 
-        def made_ready_in(pair):
-            n, i = divmod(pair, PAIRS_PER_CHUNK)
+        def made_ready_in(bank):
+            n, m = divmod(bank, TOKEN_TILES)
+            if m % RUN:
+                return []
             tiles = []
-            if n == 0 and i + 1 < PAIRS_PER_CHUNK:
-                tiles += [("x", (i + 1) * PAIR + m) for m in range(PAIR)]
-            if n + 1 < CHUNKS:
-                tiles.append(("w", n + 1, i))
+            for k in range(m, m + RUN):
+                if n == 0 and k + X_LEAD < TOKEN_TILES:
+                    tiles.append(("x", k + X_LEAD))
+            for k in range(m, m + RUN):
+                if n + 1 < CHUNKS and k % 2 == 0:
+                    tiles.append(("w", n + 1, k // 2))
             return tiles
 
         raws = {}
@@ -83,8 +88,8 @@ def tile_biboattention_pa_kernel(
 
         for tile in lead_in:
             load(tile)
-        for pair in range(PAIRS):
-            for tile in made_ready_in(pair):
+        for bank in range(BANKS):
+            for tile in made_ready_in(bank):
                 load(tile)
 
         cos_sb = const.tile([P, SEQ_TILES, HEAD_DIM], BF16)
@@ -113,7 +118,7 @@ def tile_biboattention_pa_kernel(
         table = const.tile([P, SEQ_TILES, 2, 2, HEAD_DIM], F32)
 
         def build_tables():
-          spread = flip_psum.tile([P, CHUNK], F32, name="flipped")
+          spread = acc_psum.tile([P, CHUNK], F32, name="acc")
           nc.tensor.matmul(out=spread[:], lhsT=ones[:], rhs=vectors[:], start=True, stop=True)
           norm_w = spread[:, : 2 * HEAD_DIM].rearrange("p (kind d) -> p kind d", kind=2)
           nc.vector.memset(gain[:, Q_HEADS:], 1.0)
@@ -192,93 +197,85 @@ def tile_biboattention_pa_kernel(
                     in_=grouped[:, g, :, :].rearrange("p r u -> p (r u)").bitcast(BF16),
                 )
 
-        def tiles_of(pair):
-            n, i = divmod(pair, PAIRS_PER_CHUNK)
-            return n, [i * PAIR + m for m in range(PAIR)]
-
         accs = {}
         sums = {}
         factors = {}
         prods = {}
         results = {}
 
-        def project(pair):
-            n, ms = tiles_of(pair)
+        def project(bank):
+            n, m = divmod(bank, TOKEN_TILES)
             w_codes, w_scales = w_mx[n]
-            for m in ms:
-                acc = acc_psum.tile([P, CHUNK], F32)
-                for g in range(PASSES):
-                    nc.tensor.matmul_mx(
-                        out=acc[:],
-                        lhsT=x_codes[:, m, g, :].bitcast(FP8X4),
-                        lhsT_scale=x_scales[:, m, g, :],
-                        rhs=w_codes[:, g, :].bitcast(FP8X4),
-                        rhs_scale=w_scales[:, g, :],
-                        start=(g == 0),
-                        stop=(g == PASSES - 1),
-                    )
-                accs[m, n] = acc
+            acc = acc_psum.tile([P, CHUNK], F32, name="acc")
+            for g in range(PASSES):
+                nc.tensor.matmul_mx(
+                    out=acc[:],
+                    lhsT=x_codes[:, m, g, :].bitcast(FP8X4),
+                    lhsT_scale=x_scales[:, m, g, :],
+                    rhs=w_codes[:, g, :].bitcast(FP8X4),
+                    rhs_scale=w_scales[:, g, :],
+                    start=(g == 0),
+                    stop=(g == PASSES - 1),
+                )
+            accs[bank] = acc
 
-        def square_sums(pair):
-            n, ms = tiles_of(pair)
-            sumsq = small.tile([P, PAIR, CHUNK_HEADS], F32)
-            for i, m in enumerate(ms):
-                for h in range(CHUNK_HEADS):
-                    squares = small.tile([P, HEAD_DIM], F32)
-                    nc.scalar.activation(
-                        out=squares[:],
-                        in_=accs[m, n][:, h * HEAD_DIM : (h + 1) * HEAD_DIM],
-                        func=ACT.Square,
-                        accum_out=sumsq[:, i, h : h + 1],
-                    )
-            sums[pair] = sumsq
+        def square_sums(bank):
+            sumsq = small.tile([P, CHUNK_HEADS], F32)
+            for h in range(CHUNK_HEADS):
+                squares = small.tile([P, HEAD_DIM], F32)
+                nc.scalar.activation(
+                    out=squares[:],
+                    in_=accs[bank][:, h * HEAD_DIM : (h + 1) * HEAD_DIM],
+                    func=ACT.Square,
+                    accum_out=sumsq[:, h : h + 1],
+                )
+            sums[bank] = sumsq
 
-        def make_factors(pair):
-            n, ms = tiles_of(pair)
-            rstd = small.tile([P, PAIR, CHUNK_HEADS], F32)
+        def make_factors(bank):
+            n = bank // TOKEN_TILES
+            rstd = small.tile([P, CHUNK_HEADS], F32)
             nc.scalar.activation(
-                out=rstd[:], in_=sums[pair][:], func=ACT.Abs_reciprocal_sqrt, scale=1.0 / HEAD_DIM, bias=EPS
+                out=rstd[:], in_=sums[bank][:], func=ACT.Abs_reciprocal_sqrt, scale=1.0 / HEAD_DIM, bias=EPS
             )
-            factor = small.tile([P, PAIR, CHUNK_HEADS], F32)
+            if n == Q_CHUNKS:
+                factors[bank] = rstd
+                return
+            factor = small.tile([P, CHUNK_HEADS], F32)
             nc.gpsimd.tensor_tensor(
-                out=factor[:],
-                in0=rstd[:],
-                in1=gain[:, n * CHUNK_HEADS : (n + 1) * CHUNK_HEADS].unsqueeze(1).to_broadcast([P, PAIR, CHUNK_HEADS]),
-                op=ALU.mult,
+                out=factor[:], in0=rstd[:], in1=gain[:, n * CHUNK_HEADS : (n + 1) * CHUNK_HEADS], op=ALU.mult
             )
-            factors[pair] = factor
+            factors[bank] = factor
 
-        def multiply(pair, i):
-            n, ms = tiles_of(pair)
+        def multiply(bank):
+            n, m = divmod(bank, TOKEN_TILES)
             kind = 0 if n < Q_CHUNKS else 1
-            acc = accs[ms[i], n]
             prod = prod_pool.tile([P, CHUNK_HEADS, 2, 2, HALF], F32)
             for h in range(CHUNK_HEADS):
                 nc.vector.scalar_tensor_tensor(
                     out=prod[:, h, :, :, :].rearrange("p k a d -> p k (a d)"),
-                    in0=table[:, ms[i] % SEQ_TILES, kind, :, :],
-                    scalar=factors[pair][:, i, h : h + 1],
-                    in1=acc[:, h * HEAD_DIM : (h + 1) * HEAD_DIM].unsqueeze(1).to_broadcast([P, 2, HEAD_DIM]),
+                    in0=table[:, m % SEQ_TILES, kind, :, :],
+                    scalar=factors[bank][:, h : h + 1],
+                    in1=accs[bank][:, h * HEAD_DIM : (h + 1) * HEAD_DIM].unsqueeze(1).to_broadcast([P, 2, HEAD_DIM]),
                     op0=ALU.mult,
                     op1=ALU.mult,
                 )
-            prods[pair, i] = prod
+            prods[bank] = prod
 
-        def add_and_store(pair, i):
-            n, ms = tiles_of(pair)
-            b, t = divmod(ms[i], SEQ_TILES)
+        def add_and_store(bank):
+            n, m = divmod(bank, TOKEN_TILES)
+            b, t = divmod(m, SEQ_TILES)
             if t == 0:
                 result = result_pool.tile([P, CHUNK_HEADS, SEQ_TILES, 2, HALF], F32)
                 results[0] = result
             result = results[0]
-            prod = prods[pair, i]
+            prod = prods[bank]
             nc.gpsimd.tensor_tensor(
                 out=result[:, :, t, :, :], in0=prod[:, :, 0, :, :], in1=prod[:, :, 1, ::-1, :], op=ALU.add
             )
             heads = out_0[b, n * CHUNK_HEADS : (n + 1) * CHUNK_HEADS] if n < Q_CHUNKS else out_1[b]
             rows = heads.rearrange("h (p t) d -> p h t d", t=SEQ_TILES)
-            last = pair == PAIRS - 1
-            if last or i == PAIR - 1:
+            last = bank >= BANKS - 2
+            if last or t % 2:
                 first = t if last else t - 1
                 nc.sync.dma_start(
                     out=rows[:, :, first : t + 1, :],
@@ -290,28 +287,23 @@ def tile_biboattention_pa_kernel(
             group(tile, 0)
             group(tile, 1)
             quantise(tile)
-        build_tables()
-        for pair in range(PAIRS + 1):
-            ready = made_ready_in(pair) if pair < PAIRS else []
+            if tile == lead_in[0]:
+                build_tables()
+        for step in range(BANKS + ADD_LAG):
+            ready = made_ready_in(step) if step < BANKS else []
             for tile in ready:
                 turn(tile)
+            if step < BANKS:
+                project(step)
+            for tile in ready:
                 group(tile, 0)
-                if tile == ready[0] and pair > 0:
-                    make_factors(pair - 1)
                 group(tile, 1)
-            if not ready:
-                make_factors(pair - 1)
-            if pair > 0:
-                multiply(pair - 1, 0)
-            for tile in ready[:1]:
+            if 0 <= step - 2 < BANKS:
+                add_and_store(step - 2)
+            if 0 <= step - 1 < BANKS:
+                multiply(step - 1)
+            if step < BANKS:
+                square_sums(step)
+                make_factors(step)
+            for tile in ready:
                 quantise(tile)
-            if pair > 0:
-                add_and_store(pair - 1, 0)
-                multiply(pair - 1, 1)
-            for tile in ready[1:]:
-                quantise(tile)
-            if pair > 0:
-                add_and_store(pair - 1, 1)
-            if pair < PAIRS:
-                project(pair)
-                square_sums(pair)

@@ -31,9 +31,8 @@ HEADS = Q_HEADS + KV_HEADS
 ROW_TILES = TOKEN_TILES + CHUNKS * CHUNK_HEADS
 
 X_LEAD = 2
-RUN = 2
 BANKS = CHUNKS * TOKEN_TILES
-ADD_LAG = 2
+ADD_LAG = 3
 
 FLOPS = 2 * BATCH * SEQ * HIDDEN * HEADS * HEAD_DIM
 
@@ -62,16 +61,12 @@ def tile_biboattention_pa_kernel(
 
         def made_ready_in(bank):
             n, m = divmod(bank, TOKEN_TILES)
-            if m % RUN:
-                return []
-            tiles = []
-            for k in range(m, m + RUN):
-                if n == 0 and k + X_LEAD < TOKEN_TILES:
-                    tiles.append(("x", k + X_LEAD))
-            for k in range(m, m + RUN):
-                if n + 1 < CHUNKS and k % 2 == 0:
-                    tiles.append(("w", n + 1, k // 2))
-            return tiles
+            if n == 0 and m % 2 == 0 and m + X_LEAD < TOKEN_TILES:
+                return [("x", m + X_LEAD), ("x", m + X_LEAD + 1)]
+            if n + 1 < CHUNKS and m % SEQ_TILES == SEQ_TILES - 1:
+                half = m // SEQ_TILES
+                return [("w", n + 1, 2 * half), ("w", n + 1, 2 * half + 1)]
+            return []
 
         raws = {}
 
@@ -287,7 +282,7 @@ def tile_biboattention_pa_kernel(
             group(tile, 0)
             group(tile, 1)
             quantise(tile)
-            if tile == lead_in[0]:
+            if tile == lead_in[2]:
                 build_tables()
         for step in range(BANKS + ADD_LAG):
             ready = made_ready_in(step) if step < BANKS else []
@@ -298,12 +293,13 @@ def tile_biboattention_pa_kernel(
             for tile in ready:
                 group(tile, 0)
                 group(tile, 1)
+            if 0 <= step - 3 < BANKS:
+                add_and_store(step - 3)
             if 0 <= step - 2 < BANKS:
-                add_and_store(step - 2)
+                multiply(step - 2)
             if 0 <= step - 1 < BANKS:
-                multiply(step - 1)
+                make_factors(step - 1)
             if step < BANKS:
                 square_sums(step)
-                make_factors(step)
             for tile in ready:
                 quantise(tile)

from contextlib import ExitStack
import math

import concourse.mybir as mybir
from concourse.masks import make_identity

F32 = mybir.dt.float32
BF16 = mybir.dt.bfloat16
U32 = mybir.dt.uint32
U8 = mybir.dt.uint8
FP8X4 = mybir.dt.float8_e4m3fn_x4
ACT = mybir.ActivationFunctionType
ALU = mybir.AluOpType

P = 128
BATCH, SEQ, HIDDEN = 2, 512, 2048
Q_HEADS, KV_HEADS, HEAD_DIM = 16, 4, 128
HALF = HEAD_DIM // 2
EPS = 1e-6

K_PASS = 4 * P
PASSES = HIDDEN // K_PASS
WORDS_PER_PASS = K_PASS // 2
SEQ_TILES = SEQ // P
TOKEN_TILES = BATCH * SEQ_TILES
CHUNK_HEADS = 4
CHUNK = CHUNK_HEADS * HEAD_DIM
Q_CHUNKS = Q_HEADS // CHUNK_HEADS
CHUNKS = Q_CHUNKS + KV_HEADS // CHUNK_HEADS
HEADS = Q_HEADS + KV_HEADS
ROW_TILES = TOKEN_TILES + CHUNKS * CHUNK_HEADS

X_LEAD = 2
BANKS = CHUNKS * TOKEN_TILES
ADD_LAG = 3

FLOPS = 2 * BATCH * SEQ * HIDDEN * HEADS * HEAD_DIM


def tile_biboattention_pa_kernel(
    tc, hidden_states, cos, sin, wq, wk, q_norm_w, k_norm_w, ssmax_scale, out_0, out_1
):
    nc = tc.nc
    with ExitStack() as ctx:
        const = ctx.enter_context(tc.tile_pool(name="const", bufs=1))
        raw_pool = ctx.enter_context(tc.tile_pool(name="raw", bufs=ROW_TILES))
        grouped_pool = ctx.enter_context(tc.tile_pool(name="grouped", bufs=4))
        w_pool = ctx.enter_context(tc.tile_pool(name="w_mx", bufs=2))
        small = ctx.enter_context(tc.tile_pool(name="small", bufs=4))
        prod_pool = ctx.enter_context(tc.tile_pool(name="prod", bufs=3))
        result_pool = ctx.enter_context(tc.tile_pool(name="result", bufs=3))
        flip_psum = ctx.enter_context(tc.psum_pool(name="flip_psum", bufs=4))
        acc_psum = ctx.enter_context(tc.psum_pool(name="acc_psum", bufs=4))
        ctx.enter_context(tc.manual_schedule())

        x_view = hidden_states.rearrange("b (p t) k -> b t p k", t=SEQ_TILES)
        wq_view = wq.rearrange("(n j p) k -> n j p k", j=CHUNK_HEADS, p=P)
        wk_view = wk.rearrange("(j p) k -> j p k", p=P)

        lead_in = [("w", 0, j) for j in range(CHUNK_HEADS)] + [("x", m) for m in range(X_LEAD)]

        def made_ready_in(bank):
            n, m = divmod(bank, TOKEN_TILES)
            if n == 0 and m % 2 == 0 and m + X_LEAD < TOKEN_TILES:
                return [("x", m + X_LEAD), ("x", m + X_LEAD + 1)]
            if n + 1 < CHUNKS and m % SEQ_TILES == SEQ_TILES - 1:
                half = m // SEQ_TILES
                return [("w", n + 1, 2 * half), ("w", n + 1, 2 * half + 1)]
            return []

        raws = {}

        def load(tile):
            raw = raw_pool.tile([P, HIDDEN], BF16, name="raw")
            if tile[0] == "x":
                source = x_view[tile[1] // SEQ_TILES, tile[1] % SEQ_TILES]
            elif tile[1] < Q_CHUNKS:
                source = wq_view[tile[1], tile[2]]
            else:
                source = wk_view[tile[2]]
            nc.sync.dma_start(out=raw[:], in_=source)
            raws[tile] = raw

        for tile in lead_in:
            load(tile)
        for bank in range(BANKS):
            for tile in made_ready_in(bank):
                load(tile)

        cos_sb = const.tile([P, SEQ_TILES, HEAD_DIM], BF16)
        sin_sb = const.tile([P, SEQ_TILES, HEAD_DIM], BF16)
        nc.scalar.dma_start(out=cos_sb[:], in_=cos.rearrange("(p t) d -> p t d", t=SEQ_TILES))
        nc.scalar.dma_start(out=sin_sb[:], in_=sin.rearrange("(p t) d -> p t d", t=SEQ_TILES))
        vectors = const.tile([P, CHUNK], BF16)
        nc.vector.memset(vectors[:], 0.0)
        ones = const.tile([P, P], BF16)
        nc.vector.memset(ones[:], 1.0)
        nc.scalar.dma_start(out=vectors[0:1, 0:HEAD_DIM], in_=q_norm_w.unsqueeze(0))
        nc.scalar.dma_start(out=vectors[0:1, HEAD_DIM : 2 * HEAD_DIM], in_=k_norm_w.unsqueeze(0))
        nc.scalar.dma_start(
            out=vectors[0:1, 2 * HEAD_DIM : 2 * HEAD_DIM + Q_HEADS],
            in_=ssmax_scale.rearrange("a h b c -> (a b c) h"),
        )
        ident = const.tile([P, P], F32)
        make_identity(nc, ident[:])

        one = const.tile([P, 1], F32)
        nc.vector.memset(one[:], 1.0)
        warm = const.tile([P, 1], F32)
        nc.scalar.activation(out=warm[:], in_=one[:], func=ACT.Abs_reciprocal_sqrt)

        gain = const.tile([P, HEADS], F32)
        table = const.tile([P, SEQ_TILES, 2, 2, HEAD_DIM], F32)

        def build_tables():
          spread = acc_psum.tile([P, CHUNK], F32, name="acc")
          nc.tensor.matmul(out=spread[:], lhsT=ones[:], rhs=vectors[:], start=True, stop=True)
          norm_w = spread[:, : 2 * HEAD_DIM].rearrange("p (kind d) -> p kind d", kind=2)
          nc.vector.memset(gain[:, Q_HEADS:], 1.0)
          nc.vector.tensor_scalar_mul(out=gain[:, :Q_HEADS], in0=spread[:, 2 * HEAD_DIM : 2 * HEAD_DIM + Q_HEADS], scalar1=math.log(SEQ))
          for kind in range(2):
              nc.vector.tensor_tensor(
                  out=table[:, :, kind, 0, :],
                  in0=cos_sb[:],
                  in1=norm_w[:, kind, :].unsqueeze(1).to_broadcast([P, SEQ_TILES, HEAD_DIM]),
                  op=ALU.mult,
              )
              nc.vector.tensor_tensor(
                  out=table[:, :, kind, 1, :HALF],
                  in0=sin_sb[:, :, HALF:],
                  in1=norm_w[:, kind, :HALF].unsqueeze(1).to_broadcast([P, SEQ_TILES, HALF]),
                  op=ALU.mult,
              )
              nc.vector.scalar_tensor_tensor(
                  out=table[:, :, kind, 1, HALF:],
                  in0=sin_sb[:, :, :HALF],
                  scalar=-1.0,
                  in1=norm_w[:, kind, HALF:].unsqueeze(1).to_broadcast([P, SEQ_TILES, HALF]),
                  op0=ALU.mult,
                  op1=ALU.mult,
              )

        x_codes = const.tile([P, TOKEN_TILES, PASSES, P], U32, align_bytes=64)
        x_scales = const.tile([P, TOKEN_TILES, PASSES, P], U8, align_bytes=64)

        w_mx = {}
        banks = {}
        grouped_of = {}

        def turn(tile):
            words = raws[tile][:].bitcast(F32)
            for half in range(2):
                flipped = flip_psum.tile([P, 2, 2, P], F32, name="flipped")
                for a in range(2):
                    first = (2 * half + a) * WORDS_PER_PASS
                    for u in range(2):
                        nc.tensor.transpose(
                            flipped[:, a, u, :], words[:, first + u : first + WORDS_PER_PASS : 2], ident[:]
                        )
                banks[tile, half] = flipped

        def group(tile, half):
            if half == 0:
                grouped = grouped_pool.tile([P, PASSES, P, 2], F32, align_bytes=64)
                grouped_of[tile] = grouped
            nc.scalar.copy(
                out=grouped_of[tile][:, 2 * half : 2 * half + 2, :, :],
                in_=banks[tile, half][:].rearrange("p a u r -> p a r u"),
            )

        def quantise(tile):
            grouped = grouped_of[tile]
            if tile[0] == "x":
                for g in range(0, PASSES, 2):
                    nc.vector.quantize_mx(
                        out=x_codes[:, tile[1], g : g + 2, :].rearrange("p g r -> p (g r)").bitcast(FP8X4),
                        scales=x_scales[:, tile[1], g : g + 2, :].rearrange("p g r -> p (g r)"),
                        in_=grouped[:, g : g + 2, :, :].rearrange("p g r u -> p (g r u)").bitcast(BF16),
                    )
                return
            n, j = tile[1], tile[2]
            if j == 0:
                w_codes = w_pool.tile([P, PASSES, CHUNK], U32, align_bytes=64)
                w_scales = w_pool.tile([P, PASSES, CHUNK], U8, align_bytes=64)
                w_mx[n] = (w_codes, w_scales)
            w_codes, w_scales = w_mx[n]
            rows = slice(j * P, (j + 1) * P)
            for g in range(PASSES):
                nc.vector.quantize_mx(
                    out=w_codes[:, g, rows].bitcast(FP8X4),
                    scales=w_scales[:, g, rows],
                    in_=grouped[:, g, :, :].rearrange("p r u -> p (r u)").bitcast(BF16),
                )

        accs = {}
        sums = {}
        factors = {}
        prods = {}
        results = {}

        def project(bank):
            n, m = divmod(bank, TOKEN_TILES)
            w_codes, w_scales = w_mx[n]
            acc = acc_psum.tile([P, CHUNK], F32, name="acc")
            for g in range(PASSES):
                nc.tensor.matmul_mx(
                    out=acc[:],
                    lhsT=x_codes[:, m, g, :].bitcast(FP8X4),
                    lhsT_scale=x_scales[:, m, g, :],
                    rhs=w_codes[:, g, :].bitcast(FP8X4),
                    rhs_scale=w_scales[:, g, :],
                    start=(g == 0),
                    stop=(g == PASSES - 1),
                )
            accs[bank] = acc

        def square_sums(bank):
            sumsq = small.tile([P, CHUNK_HEADS], F32)
            for h in range(CHUNK_HEADS):
                squares = small.tile([P, HEAD_DIM], F32)
                nc.scalar.activation(
                    out=squares[:],
                    in_=accs[bank][:, h * HEAD_DIM : (h + 1) * HEAD_DIM],
                    func=ACT.Square,
                    accum_out=sumsq[:, h : h + 1],
                )
            sums[bank] = sumsq

        def make_factors(bank):
            n = bank // TOKEN_TILES
            rstd = small.tile([P, CHUNK_HEADS], F32)
            nc.scalar.activation(
                out=rstd[:], in_=sums[bank][:], func=ACT.Abs_reciprocal_sqrt, scale=1.0 / HEAD_DIM, bias=EPS
            )
            if n == Q_CHUNKS:
                factors[bank] = rstd
                return
            factor = small.tile([P, CHUNK_HEADS], F32)
            nc.gpsimd.tensor_tensor(
                out=factor[:], in0=rstd[:], in1=gain[:, n * CHUNK_HEADS : (n + 1) * CHUNK_HEADS], op=ALU.mult
            )
            factors[bank] = factor

        def multiply(bank):
            n, m = divmod(bank, TOKEN_TILES)
            kind = 0 if n < Q_CHUNKS else 1
            prod = prod_pool.tile([P, CHUNK_HEADS, 2, 2, HALF], F32)
            for h in range(CHUNK_HEADS):
                nc.vector.scalar_tensor_tensor(
                    out=prod[:, h, :, :, :].rearrange("p k a d -> p k (a d)"),
                    in0=table[:, m % SEQ_TILES, kind, :, :],
                    scalar=factors[bank][:, h : h + 1],
                    in1=accs[bank][:, h * HEAD_DIM : (h + 1) * HEAD_DIM].unsqueeze(1).to_broadcast([P, 2, HEAD_DIM]),
                    op0=ALU.mult,
                    op1=ALU.mult,
                )
            prods[bank] = prod

        def add_and_store(bank):
            n, m = divmod(bank, TOKEN_TILES)
            b, t = divmod(m, SEQ_TILES)
            if t == 0:
                result = result_pool.tile([P, CHUNK_HEADS, SEQ_TILES, 2, HALF], F32)
                results[0] = result
            result = results[0]
            prod = prods[bank]
            nc.gpsimd.tensor_tensor(
                out=result[:, :, t, :, :], in0=prod[:, :, 0, :, :], in1=prod[:, :, 1, ::-1, :], op=ALU.add
            )
            heads = out_0[b, n * CHUNK_HEADS : (n + 1) * CHUNK_HEADS] if n < Q_CHUNKS else out_1[b]
            rows = heads.rearrange("h (p t) d -> p h t d", t=SEQ_TILES)
            last = bank >= BANKS - 2
            if last or t % 2:
                first = t if last else t - 1
                nc.sync.dma_start(
                    out=rows[:, :, first : t + 1, :],
                    in_=result[:, :, first : t + 1, :, :].rearrange("p h t a d -> p h t (a d)"),
                )

        for tile in lead_in:
            turn(tile)
            group(tile, 0)
            group(tile, 1)
            quantise(tile)
            if tile == lead_in[2]:
                build_tables()
        for step in range(BANKS + ADD_LAG):
            ready = made_ready_in(step) if step < BANKS else []
            for tile in ready:
                turn(tile)
            if step < BANKS:
                project(step)
            for tile in ready:
                group(tile, 0)
                group(tile, 1)
            if 0 <= step - 3 < BANKS:
                add_and_store(step - 3)
            if 0 <= step - 2 < BANKS:
                multiply(step - 2)
            if 0 <= step - 1 < BANKS:
                make_factors(step - 1)
            if step < BANKS:
                square_sums(step)
            for tile in ready:
                quantise(tile)
